import numpy as np
import ml_dtypes


def mxq(x, axis, fmt="e4m3"):
    dtype, down = {"e4m3": (ml_dtypes.float8_e4m3fn, 7), "e5m2": (ml_dtypes.float8_e5m2, 14)}[fmt]
    v = np.moveaxis(np.asarray(x, np.float32).astype(ml_dtypes.bfloat16).astype(np.float64), axis, -1)
    blocks = v.reshape(v.shape[:-1] + (-1, 32))
    amax = np.abs(blocks).max(-1, keepdims=True)
    byte = np.maximum(np.where(amax > 0, np.frexp(amax)[1] - 1 + 127, 0) - down, 1)
    scale = np.exp2(byte - 127.0)
    codes = (blocks / scale).astype(np.float32).astype(dtype).astype(np.float64)
    return np.moveaxis((codes * scale).reshape(v.shape), -1, axis)


WIDE = False


def mx_kscale(k):
    if not WIDE:
        return np.ones(k)
    levels = np.array([10, -10, 5, -5, 0])
    a = np.random.permutation(np.resize(levels, k // 512 * 4)).reshape(k // 512, 4)
    idx = np.arange(k)
    return np.exp2(a[idx // 512, idx % 128 // 32])


BF16 = ml_dtypes.bfloat16


def bf(x):
    return np.asarray(x, np.float32).astype(BF16)


def f64(x):
    return np.asarray(x).astype(np.float64)


B, D, U = 128, 512, 512


def hard_sigmoid(v):
    return np.clip(0.2 * v + 0.5, 0.0, 1.0)


def setup_inputs():
    s = mx_kscale(D)
    return {"inputs": bf(np.random.standard_normal((B, D)) * s),
            "h_tm1": bf(np.random.standard_normal((B, U))),
            "kernel": bf(np.random.standard_normal((D, 3 * U)) * 0.64 / np.sqrt(D) / s[:, None]),
            "recurrent_kernel": bf(np.random.standard_normal((U, 3 * U)) * 0.64 / np.sqrt(U)),
            "bias": bf(np.random.standard_normal((2, 3 * U)) * 0.2)}


def reference(inputs, h_tm1, kernel, recurrent_kernel, bias):
    units = recurrent_kernel.shape[0]
    h_prev = f64(h_tm1)
    b = f64(bias)
    input_bias, recurrent_bias = b[0], b[1]

    matrix_x = (mxq(f64(inputs), 1, "e4m3") @ mxq(f64(kernel), 0, "e4m3")) + input_bias
    x_z, x_r, x_h = np.split(matrix_x, 3, axis=-1)

    matrix_inner = (mxq(h_prev, 1, "e4m3") @ mxq(f64(recurrent_kernel), 0, "e4m3")) + recurrent_bias
    rec_z = matrix_inner[:, :units]
    rec_r = matrix_inner[:, units:2 * units]
    rec_h = matrix_inner[:, 2 * units:]

    z = hard_sigmoid(x_z + rec_z)
    r = hard_sigmoid(x_r + rec_r)
    hh = np.tanh(x_h + r * rec_h)
    h = z * h_prev + (1.0 - z) * hh
    return h

@@ -1,0 +1,225 @@
+from contextlib import ExitStack
+
+import concourse.mybir as mybir
+from concourse.masks import make_identity
+
+BF16 = mybir.dt.bfloat16
+F32 = mybir.dt.float32
+U32 = mybir.dt.uint32
+U8 = mybir.dt.uint8
+FP8X4 = mybir.dt.float8_e4m3fn_x4
+ALU = mybir.AluOpType
+ACT = mybir.ActivationFunctionType
+
+P = 128
+PACK = 4
+B = 128
+U = 512
+UNIT_TILES = U // P
+HALF = U // 2
+HALF_TILES = UNIT_TILES // 2
+
+X_SIDE, H_SIDE = 0, 1
+GATE_Z, GATE_R, GATE_C = 0, 1, 2
+
+FLOPS = 2 * 2 * B * U * 3 * U
+
+
+def tile_gruskipcell_s_kernel(tc, inputs, h_tm1, kernel, recurrent_kernel, bias, out):
+    nc = tc.nc
+    weights = (kernel, recurrent_kernel)
+
+    with ExitStack() as ctx:
+        keep = ctx.enter_context(tc.tile_pool(name="keep", bufs=1))
+        psum = ctx.enter_context(tc.psum_pool(name="psum", bufs=8))
+
+        x_sb = keep.tile([B, U], BF16)
+        h_sb = keep.tile([B, U], BF16)
+        nc.sync.dma_start(out=x_sb[:], in_=inputs)
+        nc.sync.dma_start(out=h_sb[:], in_=h_tm1)
+
+        raw = {}
+        for side, gate in (
+            (X_SIDE, GATE_R),
+            (H_SIDE, GATE_R),
+            (H_SIDE, GATE_C),
+            (X_SIDE, GATE_C),
+            (X_SIDE, GATE_Z),
+            (H_SIDE, GATE_Z),
+        ):
+            raw[(side, gate)] = keep.tile([P, PACK, U], BF16, name="raw_%d_%d" % (side, gate))
+            nc.sync.dma_start(
+                out=raw[(side, gate)][:],
+                in_=weights[side][:, gate * U : (gate + 1) * U].rearrange("(t p) n -> p t n", p=P),
+            )
+
+        bias_rows = keep.tile([P, P], BF16)
+        nc.gpsimd.memset(bias_rows[:], 0.0)
+        nc.gpsimd.dma_start(
+            out=bias_rows[0 : 2 * 3 * UNIT_TILES, :], in_=bias.rearrange("i (c p) -> (i c) p", p=P)
+        )
+        ident_bf = keep.tile([P, P], BF16)
+        make_identity(nc, ident_bf[:])
+        ident_f32 = keep.tile([P, P], F32)
+        make_identity(nc, ident_f32[:])
+
+        warm_in = keep.tile([P, 1], F32)
+        warm_out = keep.tile([P, 1], F32)
+        nc.vector.memset(warm_in[:], 0.0)
+        nc.scalar.activation(out=warm_out[:], in_=warm_in[:], func=ACT.Tanh)
+
+        x_t = psum.tile([P, PACK, B], BF16, tag="bank")
+        h_t = psum.tile([P, PACK, B], BF16, tag="bank")
+        bias_t = psum.tile([P, P], BF16, tag="bank")
+        for t in range(PACK):
+            nc.tensor.transpose(x_t[:, t, :], x_sb[:, t * P : (t + 1) * P], ident_bf[:])
+        for t in range(PACK):
+            nc.tensor.transpose(h_t[:, t, :], h_sb[:, t * P : (t + 1) * P], ident_bf[:])
+        nc.tensor.transpose(bias_t[:], bias_rows[:], ident_bf[:])
+
+        act_grouped = keep.tile([P, 2, B, PACK], BF16, align_bytes=64)
+        act_codes = keep.tile([P, 2, B], U32, align_bytes=64)
+        act_scales = keep.tile([P, 2, B], U8, align_bytes=64)
+        nc.vector.tensor_copy(out=act_grouped[:, X_SIDE, :, :], in_=x_t[:].rearrange("p t b -> p b t"))
+        nc.scalar.copy(out=act_grouped[:, H_SIDE, :, :], in_=h_t[:].rearrange("p t b -> p b t"))
+        nc.vector.quantize_mx(
+            out=act_codes[:].rearrange("p s b -> p (s b)").bitcast(FP8X4),
+            scales=act_scales[:].rearrange("p s b -> p (s b)"),
+            in_=act_grouped[:].rearrange("p s b t -> p (s b t)"),
+        )
+
+        bias_cols = keep.tile([P, 2 * 3 * UNIT_TILES], F32)
+        nc.vector.tensor_copy(out=bias_cols[:], in_=bias_t[:, 0 : 2 * 3 * UNIT_TILES])
+        gate_shift = keep.tile([P, 2 * UNIT_TILES], F32)
+        nc.vector.scalar_tensor_tensor(
+            out=gate_shift[:],
+            in0=bias_cols[:, 0 : 2 * UNIT_TILES],
+            scalar=2.5,
+            in1=bias_cols[:, 3 * UNIT_TILES : 5 * UNIT_TILES],
+            op0=ALU.add,
+            op1=ALU.add,
+        )
+        x_cand_bias = bias_cols[:, 2 * UNIT_TILES : 3 * UNIT_TILES]
+        rec_cand_bias = keep.tile([P, UNIT_TILES], F32)
+        nc.vector.tensor_scalar_mul(
+            out=rec_cand_bias[:], in0=bias_cols[:, 5 * UNIT_TILES : 6 * UNIT_TILES], scalar1=0.2
+        )
+
+        w_codes = keep.tile([P, 2, 3 * U], U32, align_bytes=64)
+        w_scales = keep.tile([P, 2, 3 * U], U8, align_bytes=64)
+
+        def quantise_third(side, gate):
+            grouped = keep.tile([P, U, PACK], BF16, align_bytes=64, name="grouped_%d_%d" % (side, gate))
+            for half, copy in enumerate((nc.vector.tensor_copy, nc.scalar.copy)):
+                cols = slice(half * HALF, (half + 1) * HALF)
+                copy(
+                    out=grouped[:, cols, :].rearrange("p (c i) t -> p c t i", i=4),
+                    in_=raw[(side, gate)][:, :, cols].rearrange("p t (c i) -> p c t i", i=4),
+                )
+            for half in range(2):
+                cols = slice(half * HALF, (half + 1) * HALF)
+                w_cols = slice(gate * U + half * HALF, gate * U + (half + 1) * HALF)
+                nc.vector.quantize_mx(
+                    out=w_codes[:, side, w_cols].bitcast(FP8X4),
+                    scales=w_scales[:, side, w_cols],
+                    in_=grouped[:, cols, :].rearrange("p c t -> p (c t)"),
+                )
+
+        def product(acc, sides, gate, ut):
+            w_cols = slice(gate * U + ut * P, gate * U + (ut + 1) * P)
+            for side in sides:
+                nc.tensor.matmul_mx(
+                    out=acc,
+                    lhsT=w_codes[:, side, w_cols].bitcast(FP8X4),
+                    lhsT_scale=w_scales[:, side, w_cols],
+                    rhs=act_codes[:, side, :].bitcast(FP8X4),
+                    rhs_scale=act_scales[:, side, :],
+                    start=(side == sides[0]),
+                    stop=(side == sides[-1]),
+                )
+
+        quantise_third(X_SIDE, GATE_R)
+        quantise_third(H_SIDE, GATE_R)
+        acc_r = psum.tile([P, UNIT_TILES, B], F32, tag="bank")
+        r5 = keep.tile([P, UNIT_TILES, B], F32)
+        for ut in range(UNIT_TILES):
+            product(acc_r[:, ut, :], (X_SIDE, H_SIDE), GATE_R, ut)
+        for ut in range(UNIT_TILES):
+            nc.scalar.activation(
+                out=r5[:, ut, :],
+                in_=acc_r[:, ut, :],
+                func=ACT.Relu,
+                bias=gate_shift[:, UNIT_TILES + ut : UNIT_TILES + ut + 1],
+                scale=1.0,
+            )
+
+        quantise_third(H_SIDE, GATE_C)
+        acc_rec = psum.tile([P, UNIT_TILES, B], F32, tag="bank")
+        rec_fifth = keep.tile([P, UNIT_TILES, B], F32)
+        for ut in range(UNIT_TILES):
+            product(acc_rec[:, ut, :], (H_SIDE,), GATE_C, ut)
+        for ut in range(UNIT_TILES):
+            nc.scalar.activation(
+                out=rec_fifth[:, ut, :],
+                in_=acc_rec[:, ut, :],
+                func=ACT.Identity,
+                bias=rec_cand_bias[:, ut : ut + 1],
+                scale=0.2,
+            )
+        gated = keep.tile([P, UNIT_TILES, B], F32)
+        nc.vector.scalar_tensor_tensor(
+            out=gated[:], in0=r5[:], scalar=5.0, in1=rec_fifth[:], op0=ALU.min, op1=ALU.mult
+        )
+
+        quantise_third(X_SIDE, GATE_C)
+        acc_x = psum.tile([P, UNIT_TILES, B], F32, tag="bank")
+        for ut in range(UNIT_TILES):
+            product(acc_x[:, ut, :], (X_SIDE,), GATE_C, ut)
+        pre = keep.tile([P, UNIT_TILES, B], F32)
+        nc.vector.tensor_tensor(out=pre[:], in0=acc_x[:], in1=gated[:], op=ALU.add)
+        hh = keep.tile([P, UNIT_TILES, B], F32)
+        for ut in range(UNIT_TILES):
+            nc.scalar.activation(
+                out=hh[:, ut, :],
+                in_=pre[:, ut, :],
+                func=ACT.Tanh,
+                bias=x_cand_bias[:, ut : ut + 1],
+                scale=1.0,
+            )
+        diff = keep.tile([P, UNIT_TILES, B], F32)
+        nc.vector.tensor_tensor(out=diff[:], in0=h_t[:], in1=hh[:], op=ALU.subtract)
+
+        quantise_third(X_SIDE, GATE_Z)
+        quantise_third(H_SIDE, GATE_Z)
+        z5 = keep.tile([P, UNIT_TILES, B], F32)
+        moved = keep.tile([P, UNIT_TILES, B], F32)
+        new_h = keep.tile([P, UNIT_TILES, B], F32)
+        out_sb = keep.tile([B, U], F32)
+        for half, copy in enumerate((nc.scalar.copy, nc.vector.tensor_copy)):
+            tiles = slice(half * HALF_TILES, (half + 1) * HALF_TILES)
+            acc_z = psum.tile([P, HALF_TILES, B], F32, tag="bank")
+            for i in range(HALF_TILES):
+                product(acc_z[:, i, :], (X_SIDE, H_SIDE), GATE_Z, half * HALF_TILES + i)
+            for i in range(HALF_TILES):
+                ut = half * HALF_TILES + i
+                nc.scalar.activation(
+                    out=z5[:, ut, :],
+                    in_=acc_z[:, i, :],
+                    func=ACT.Relu,
+                    bias=gate_shift[:, ut : ut + 1],
+                    scale=1.0,
+                )
+            nc.vector.scalar_tensor_tensor(
+                out=moved[:, tiles, :], in0=z5[:, tiles, :], scalar=5.0, in1=diff[:, tiles, :],
+                op0=ALU.min, op1=ALU.mult,
+            )
+            nc.vector.scalar_tensor_tensor(
+                out=new_h[:, tiles, :], in0=moved[:, tiles, :], scalar=0.2, in1=hh[:, tiles, :],
+                op0=ALU.mult, op1=ALU.add,
+            )
+            back = psum.tile([B, HALF_TILES, P], F32, tag="bank")
+            for i in range(HALF_TILES):
+                nc.tensor.transpose(back[:, i, :], new_h[:, half * HALF_TILES + i, :], ident_f32[:])
+            cols = slice(half * HALF, (half + 1) * HALF)
+            copy(out=out_sb[:, cols], in_=back[:].rearrange("b i p -> b (i p)"))
+            nc.sync.dma_start(out=out[:, cols], in_=out_sb[:, cols])

@@ -31,31 +31,91 @@ def tile_gruskipcell_s_kernel(tc, inputs, h_tm1, kernel, recurrent_kernel, bias,
 
     with ExitStack() as ctx:
         keep = ctx.enter_context(tc.tile_pool(name="keep", bufs=1))
-        psum = ctx.enter_context(tc.psum_pool(name="psum", bufs=8))
-
-        x_sb = keep.tile([B, U], BF16)
-        h_sb = keep.tile([B, U], BF16)
-        nc.sync.dma_start(out=x_sb[:], in_=inputs)
-        nc.sync.dma_start(out=h_sb[:], in_=h_tm1)
+        psum_h = ctx.enter_context(tc.psum_pool(name="psum_h", bufs=1))
+        psum = ctx.enter_context(tc.psum_pool(name="psum", bufs=7))
+        ctx.enter_context(tc.manual_schedule())
 
         raw = {}
-        for side, gate in (
-            (X_SIDE, GATE_R),
-            (H_SIDE, GATE_R),
-            (H_SIDE, GATE_C),
-            (X_SIDE, GATE_C),
-            (X_SIDE, GATE_Z),
-            (H_SIDE, GATE_Z),
-        ):
+        grouped = {}
+        w_codes = keep.tile([P, 2, 3 * U], U32, align_bytes=64)
+        w_scales = keep.tile([P, 2, 3 * U], U8, align_bytes=64)
+        act_grouped = keep.tile([P, 2, B, PACK], BF16, align_bytes=64)
+        act_codes = keep.tile([P, 2, B], U32, align_bytes=64)
+        act_scales = keep.tile([P, 2, B], U8, align_bytes=64)
+
+        def load_third(side, gate):
             raw[(side, gate)] = keep.tile([P, PACK, U], BF16, name="raw_%d_%d" % (side, gate))
             nc.sync.dma_start(
                 out=raw[(side, gate)][:],
                 in_=weights[side][:, gate * U : (gate + 1) * U].rearrange("(t p) n -> p t n", p=P),
             )
 
+        def regroup_third(side, gate):
+            grouped[(side, gate)] = keep.tile(
+                [P, U, PACK], BF16, align_bytes=64, name="grouped_%d_%d" % (side, gate)
+            )
+            for half, copy in enumerate((nc.vector.tensor_copy, nc.scalar.copy)):
+                cols = slice(half * HALF, (half + 1) * HALF)
+                copy(
+                    out=grouped[(side, gate)][:, cols, :].rearrange("p (c i) t -> p c t i", i=4),
+                    in_=raw[(side, gate)][:, :, cols].rearrange("p t (c i) -> p c t i", i=4),
+                )
+
+        def quantise_third(side, gate):
+            for half in range(2):
+                cols = slice(half * HALF, (half + 1) * HALF)
+                w_cols = slice(gate * U + half * HALF, gate * U + (half + 1) * HALF)
+                nc.vector.quantize_mx(
+                    out=w_codes[:, side, w_cols].bitcast(FP8X4),
+                    scales=w_scales[:, side, w_cols],
+                    in_=grouped[(side, gate)][:, cols, :].rearrange("p c t -> p (c t)"),
+                )
+
+        def products(sides, gate, name):
+            acc = []
+            for half in range(2):
+                acc.append(psum.tile([P, HALF_TILES, B], F32, tag="bank", name="%s_%d" % (name, half)))
+                for i in range(HALF_TILES):
+                    first = gate * U + half * HALF + i * P
+                    for side in sides:
+                        nc.tensor.matmul_mx(
+                            out=acc[half][:, i, :],
+                            lhsT=w_codes[:, side, first : first + P].bitcast(FP8X4),
+                            lhsT_scale=w_scales[:, side, first : first + P],
+                            rhs=act_codes[:, side, :].bitcast(FP8X4),
+                            rhs_scale=act_scales[:, side, :],
+                            start=(side == sides[0]),
+                            stop=(side == sides[-1]),
+                        )
+            return acc
+
+        def scalar_function(dst, src_halves, func, bias_columns, scale):
+            for ut in range(UNIT_TILES):
+                nc.scalar.activation(
+                    out=dst[:, ut, :],
+                    in_=src_halves[ut // HALF_TILES][:, ut % HALF_TILES, :],
+                    func=func,
+                    bias=bias_columns[:, ut : ut + 1],
+                    scale=scale,
+                )
+
+        def halves(tile):
+            return [tile[:, half * HALF_TILES : (half + 1) * HALF_TILES, :] for half in range(2)]
+
+        x_sb = keep.tile([B, U], BF16)
+        h_sb = keep.tile([B, U], BF16)
+        load_third(X_SIDE, GATE_R)
+        nc.sync.dma_start(out=x_sb[:], in_=inputs)
+        nc.sync.dma_start(out=h_sb[:], in_=h_tm1)
+        load_third(H_SIDE, GATE_R)
+        load_third(H_SIDE, GATE_C)
+        load_third(X_SIDE, GATE_C)
+        load_third(X_SIDE, GATE_Z)
+        load_third(H_SIDE, GATE_Z)
+
         bias_rows = keep.tile([P, P], BF16)
-        nc.gpsimd.memset(bias_rows[:], 0.0)
-        nc.gpsimd.dma_start(
+        nc.vector.memset(bias_rows[:], 0.0)
+        nc.scalar.dma_start(
             out=bias_rows[0 : 2 * 3 * UNIT_TILES, :], in_=bias.rearrange("i (c p) -> (i c) p", p=P)
         )
         ident_bf = keep.tile([P, P], BF16)
@@ -68,25 +128,26 @@ def tile_gruskipcell_s_kernel(tc, inputs, h_tm1, kernel, recurrent_kernel, bias,
         nc.vector.memset(warm_in[:], 0.0)
         nc.scalar.activation(out=warm_out[:], in_=warm_in[:], func=ACT.Tanh)
 
+        regroup_third(X_SIDE, GATE_R)
+
         x_t = psum.tile([P, PACK, B], BF16, tag="bank")
-        h_t = psum.tile([P, PACK, B], BF16, tag="bank")
+        h_t = psum_h.tile([P, PACK, B], BF16)
         bias_t = psum.tile([P, P], BF16, tag="bank")
         for t in range(PACK):
             nc.tensor.transpose(x_t[:, t, :], x_sb[:, t * P : (t + 1) * P], ident_bf[:])
         for t in range(PACK):
             nc.tensor.transpose(h_t[:, t, :], h_sb[:, t * P : (t + 1) * P], ident_bf[:])
         nc.tensor.transpose(bias_t[:], bias_rows[:], ident_bf[:])
-
-        act_grouped = keep.tile([P, 2, B, PACK], BF16, align_bytes=64)
-        act_codes = keep.tile([P, 2, B], U32, align_bytes=64)
-        act_scales = keep.tile([P, 2, B], U8, align_bytes=64)
         nc.vector.tensor_copy(out=act_grouped[:, X_SIDE, :, :], in_=x_t[:].rearrange("p t b -> p b t"))
         nc.scalar.copy(out=act_grouped[:, H_SIDE, :, :], in_=h_t[:].rearrange("p t b -> p b t"))
+
+        regroup_third(H_SIDE, GATE_R)
         nc.vector.quantize_mx(
             out=act_codes[:].rearrange("p s b -> p (s b)").bitcast(FP8X4),
             scales=act_scales[:].rearrange("p s b -> p (s b)"),
             in_=act_grouped[:].rearrange("p s b t -> p (s b t)"),
         )
+        quantise_third(X_SIDE, GATE_R)
 
         bias_cols = keep.tile([P, 2 * 3 * UNIT_TILES], F32)
         nc.vector.tensor_copy(out=bias_cols[:], in_=bias_t[:, 0 : 2 * 3 * UNIT_TILES])
@@ -99,122 +160,64 @@ def tile_gruskipcell_s_kernel(tc, inputs, h_tm1, kernel, recurrent_kernel, bias,
             op0=ALU.add,
             op1=ALU.add,
         )
-        x_cand_bias = bias_cols[:, 2 * UNIT_TILES : 3 * UNIT_TILES]
         rec_cand_bias = keep.tile([P, UNIT_TILES], F32)
         nc.vector.tensor_scalar_mul(
             out=rec_cand_bias[:], in0=bias_cols[:, 5 * UNIT_TILES : 6 * UNIT_TILES], scalar1=0.2
         )
 
-        w_codes = keep.tile([P, 2, 3 * U], U32, align_bytes=64)
-        w_scales = keep.tile([P, 2, 3 * U], U8, align_bytes=64)
-
-        def quantise_third(side, gate):
-            grouped = keep.tile([P, U, PACK], BF16, align_bytes=64, name="grouped_%d_%d" % (side, gate))
-            for half, copy in enumerate((nc.vector.tensor_copy, nc.scalar.copy)):
-                cols = slice(half * HALF, (half + 1) * HALF)
-                copy(
-                    out=grouped[:, cols, :].rearrange("p (c i) t -> p c t i", i=4),
-                    in_=raw[(side, gate)][:, :, cols].rearrange("p t (c i) -> p c t i", i=4),
-                )
-            for half in range(2):
-                cols = slice(half * HALF, (half + 1) * HALF)
-                w_cols = slice(gate * U + half * HALF, gate * U + (half + 1) * HALF)
-                nc.vector.quantize_mx(
-                    out=w_codes[:, side, w_cols].bitcast(FP8X4),
-                    scales=w_scales[:, side, w_cols],
-                    in_=grouped[:, cols, :].rearrange("p c t -> p (c t)"),
-                )
-
-        def product(acc, sides, gate, ut):
-            w_cols = slice(gate * U + ut * P, gate * U + (ut + 1) * P)
-            for side in sides:
-                nc.tensor.matmul_mx(
-                    out=acc,
-                    lhsT=w_codes[:, side, w_cols].bitcast(FP8X4),
-                    lhsT_scale=w_scales[:, side, w_cols],
-                    rhs=act_codes[:, side, :].bitcast(FP8X4),
-                    rhs_scale=act_scales[:, side, :],
-                    start=(side == sides[0]),
-                    stop=(side == sides[-1]),
-                )
-
-        quantise_third(X_SIDE, GATE_R)
+        regroup_third(H_SIDE, GATE_C)
         quantise_third(H_SIDE, GATE_R)
-        acc_r = psum.tile([P, UNIT_TILES, B], F32, tag="bank")
-        r5 = keep.tile([P, UNIT_TILES, B], F32)
-        for ut in range(UNIT_TILES):
-            product(acc_r[:, ut, :], (X_SIDE, H_SIDE), GATE_R, ut)
-        for ut in range(UNIT_TILES):
-            nc.scalar.activation(
-                out=r5[:, ut, :],
-                in_=acc_r[:, ut, :],
-                func=ACT.Relu,
-                bias=gate_shift[:, UNIT_TILES + ut : UNIT_TILES + ut + 1],
-                scale=1.0,
-            )
-
+        acc_r = products((X_SIDE, H_SIDE), GATE_R, "acc_r")
+        regroup_third(X_SIDE, GATE_C)
         quantise_third(H_SIDE, GATE_C)
-        acc_rec = psum.tile([P, UNIT_TILES, B], F32, tag="bank")
-        rec_fifth = keep.tile([P, UNIT_TILES, B], F32)
-        for ut in range(UNIT_TILES):
-            product(acc_rec[:, ut, :], (H_SIDE,), GATE_C, ut)
-        for ut in range(UNIT_TILES):
-            nc.scalar.activation(
-                out=rec_fifth[:, ut, :],
-                in_=acc_rec[:, ut, :],
-                func=ACT.Identity,
-                bias=rec_cand_bias[:, ut : ut + 1],
-                scale=0.2,
-            )
-        gated = keep.tile([P, UNIT_TILES, B], F32)
-        nc.vector.scalar_tensor_tensor(
-            out=gated[:], in0=r5[:], scalar=5.0, in1=rec_fifth[:], op0=ALU.min, op1=ALU.mult
-        )
+        acc_rec = products((H_SIDE,), GATE_C, "acc_rec")
 
+        r5 = keep.tile([P, UNIT_TILES, B], F32)
+        scalar_function(r5, acc_r, ACT.Relu, gate_shift[:, UNIT_TILES : 2 * UNIT_TILES], 1.0)
+        rec_fifth = keep.tile([P, UNIT_TILES, B], F32)
+        scalar_function(rec_fifth, acc_rec, ACT.Identity, rec_cand_bias, 0.2)
+
+        regroup_third(X_SIDE, GATE_Z)
         quantise_third(X_SIDE, GATE_C)
-        acc_x = psum.tile([P, UNIT_TILES, B], F32, tag="bank")
-        for ut in range(UNIT_TILES):
-            product(acc_x[:, ut, :], (X_SIDE,), GATE_C, ut)
-        pre = keep.tile([P, UNIT_TILES, B], F32)
-        nc.vector.tensor_tensor(out=pre[:], in0=acc_x[:], in1=gated[:], op=ALU.add)
-        hh = keep.tile([P, UNIT_TILES, B], F32)
-        for ut in range(UNIT_TILES):
-            nc.scalar.activation(
-                out=hh[:, ut, :],
-                in_=pre[:, ut, :],
-                func=ACT.Tanh,
-                bias=x_cand_bias[:, ut : ut + 1],
-                scale=1.0,
+        acc_x = products((X_SIDE,), GATE_C, "acc_x")
+        regroup_third(H_SIDE, GATE_Z)
+
+        gated = keep.tile([P, UNIT_TILES, B], F32)
+        for half in range(2):
+            nc.vector.scalar_tensor_tensor(
+                out=halves(gated)[half], in0=halves(r5)[half], scalar=5.0, in1=halves(rec_fifth)[half],
+                op0=ALU.min, op1=ALU.mult,
             )
-        diff = keep.tile([P, UNIT_TILES, B], F32)
-        nc.vector.tensor_tensor(out=diff[:], in0=h_t[:], in1=hh[:], op=ALU.subtract)
+        pre = keep.tile([P, UNIT_TILES, B], F32)
+        for half in range(2):
+            nc.vector.tensor_tensor(
+                out=halves(pre)[half], in0=acc_x[half][:], in1=halves(gated)[half], op=ALU.add
+            )
 
         quantise_third(X_SIDE, GATE_Z)
         quantise_third(H_SIDE, GATE_Z)
+        acc_z = products((X_SIDE, H_SIDE), GATE_Z, "acc_z")
+
+        hh = keep.tile([P, UNIT_TILES, B], F32)
+        scalar_function(hh, halves(pre), ACT.Tanh, bias_cols[:, 2 * UNIT_TILES : 3 * UNIT_TILES], 1.0)
+        diff = keep.tile([P, UNIT_TILES, B], F32)
+        for half in range(2):
+            nc.vector.tensor_tensor(
+                out=halves(diff)[half], in0=halves(h_t)[half], in1=halves(hh)[half], op=ALU.subtract
+            )
+
         z5 = keep.tile([P, UNIT_TILES, B], F32)
+        scalar_function(z5, acc_z, ACT.Relu, gate_shift[:, 0:UNIT_TILES], 1.0)
         moved = keep.tile([P, UNIT_TILES, B], F32)
         new_h = keep.tile([P, UNIT_TILES, B], F32)
         out_sb = keep.tile([B, U], F32)
         for half, copy in enumerate((nc.scalar.copy, nc.vector.tensor_copy)):
-            tiles = slice(half * HALF_TILES, (half + 1) * HALF_TILES)
-            acc_z = psum.tile([P, HALF_TILES, B], F32, tag="bank")
-            for i in range(HALF_TILES):
-                product(acc_z[:, i, :], (X_SIDE, H_SIDE), GATE_Z, half * HALF_TILES + i)
-            for i in range(HALF_TILES):
-                ut = half * HALF_TILES + i
-                nc.scalar.activation(
-                    out=z5[:, ut, :],
-                    in_=acc_z[:, i, :],
-                    func=ACT.Relu,
-                    bias=gate_shift[:, ut : ut + 1],
-                    scale=1.0,
-                )
             nc.vector.scalar_tensor_tensor(
-                out=moved[:, tiles, :], in0=z5[:, tiles, :], scalar=5.0, in1=diff[:, tiles, :],
+                out=halves(moved)[half], in0=halves(z5)[half], scalar=5.0, in1=halves(diff)[half],
                 op0=ALU.min, op1=ALU.mult,
             )
             nc.vector.scalar_tensor_tensor(
-                out=new_h[:, tiles, :], in0=moved[:, tiles, :], scalar=0.2, in1=hh[:, tiles, :],
+                out=halves(new_h)[half], in0=halves(moved)[half], scalar=0.2, in1=halves(hh)[half],
                 op0=ALU.mult, op1=ALU.add,
             )
             back = psum.tile([B, HALF_TILES, P], F32, tag="bank")

@@ -31,8 +31,7 @@ def tile_gruskipcell_s_kernel(tc, inputs, h_tm1, kernel, recurrent_kernel, bias,
 
     with ExitStack() as ctx:
         keep = ctx.enter_context(tc.tile_pool(name="keep", bufs=1))
-        psum_h = ctx.enter_context(tc.psum_pool(name="psum_h", bufs=1))
-        psum = ctx.enter_context(tc.psum_pool(name="psum", bufs=7))
+        psum = ctx.enter_context(tc.psum_pool(name="psum", bufs=8))
         ctx.enter_context(tc.manual_schedule())
 
         raw = {}
@@ -99,6 +98,16 @@ def tile_gruskipcell_s_kernel(tc, inputs, h_tm1, kernel, recurrent_kernel, bias,
                     scale=scale,
                 )
 
+        def batch_rows(src, name):
+            rows = []
+            for half in range(2):
+                rows.append(psum.tile([B, HALF], F32, tag="bank", name="%s_%d" % (name, half)))
+                for i in range(HALF_TILES):
+                    nc.tensor.transpose(
+                        rows[half][:, i * P : (i + 1) * P], src[:, half * HALF_TILES + i, :], ident_f32[:]
+                    )
+            return rows
+
         def halves(tile):
             return [tile[:, half * HALF_TILES : (half + 1) * HALF_TILES, :] for half in range(2)]
 
@@ -131,7 +140,7 @@ def tile_gruskipcell_s_kernel(tc, inputs, h_tm1, kernel, recurrent_kernel, bias,
         regroup_third(X_SIDE, GATE_R)
 
         x_t = psum.tile([P, PACK, B], BF16, tag="bank")
-        h_t = psum_h.tile([P, PACK, B], BF16)
+        h_t = psum.tile([P, PACK, B], BF16, tag="bank")
         bias_t = psum.tile([P, P], BF16, tag="bank")
         for t in range(PACK):
             nc.tensor.transpose(x_t[:, t, :], x_sb[:, t * P : (t + 1) * P], ident_bf[:])
@@ -200,29 +209,27 @@ def tile_gruskipcell_s_kernel(tc, inputs, h_tm1, kernel, recurrent_kernel, bias,
 
         hh = keep.tile([P, UNIT_TILES, B], F32)
         scalar_function(hh, halves(pre), ACT.Tanh, bias_cols[:, 2 * UNIT_TILES : 3 * UNIT_TILES], 1.0)
-        diff = keep.tile([P, UNIT_TILES, B], F32)
-        for half in range(2):
-            nc.vector.tensor_tensor(
-                out=halves(diff)[half], in0=halves(h_t)[half], in1=halves(hh)[half], op=ALU.subtract
-            )
-
         z5 = keep.tile([P, UNIT_TILES, B], F32)
         scalar_function(z5, acc_z, ACT.Relu, gate_shift[:, 0:UNIT_TILES], 1.0)
-        moved = keep.tile([P, UNIT_TILES, B], F32)
-        new_h = keep.tile([P, UNIT_TILES, B], F32)
+
+        hh_rows = batch_rows(hh, "hh_rows")
+        diff = keep.tile([B, U], F32)
+        for half in range(2):
+            cols = slice(half * HALF, (half + 1) * HALF)
+            nc.vector.tensor_tensor(
+                out=diff[:, cols], in0=h_sb[:, cols], in1=hh_rows[half][:], op=ALU.subtract
+            )
+        z5_rows = batch_rows(z5, "z5_rows")
+        moved = keep.tile([B, U], F32)
         out_sb = keep.tile([B, U], F32)
-        for half, copy in enumerate((nc.scalar.copy, nc.vector.tensor_copy)):
+        for half in range(2):
+            cols = slice(half * HALF, (half + 1) * HALF)
             nc.vector.scalar_tensor_tensor(
-                out=halves(moved)[half], in0=halves(z5)[half], scalar=5.0, in1=halves(diff)[half],
+                out=moved[:, cols], in0=z5_rows[half][:], scalar=5.0, in1=diff[:, cols],
                 op0=ALU.min, op1=ALU.mult,
             )
             nc.vector.scalar_tensor_tensor(
-                out=halves(new_h)[half], in0=halves(moved)[half], scalar=0.2, in1=halves(hh)[half],
+                out=out_sb[:, cols], in0=moved[:, cols], scalar=0.2, in1=hh_rows[half][:],
                 op0=ALU.mult, op1=ALU.add,
             )
-            back = psum.tile([B, HALF_TILES, P], F32, tag="bank")
-            for i in range(HALF_TILES):
-                nc.tensor.transpose(back[:, i, :], new_h[:, half * HALF_TILES + i, :], ident_f32[:])
-            cols = slice(half * HALF, (half + 1) * HALF)
-            copy(out=out_sb[:, cols], in_=back[:].rearrange("b i p -> b (i p)"))
             nc.sync.dma_start(out=out[:, cols], in_=out_sb[:, cols])

@@ -116,17 +116,17 @@ def tile_gruskipcell_s_kernel(tc, inputs, h_tm1, kernel, recurrent_kernel, bias,
         load_third(X_SIDE, GATE_R)
         nc.sync.dma_start(out=x_sb[:], in_=inputs)
         nc.sync.dma_start(out=h_sb[:], in_=h_tm1)
+        bias_rows = keep.tile([P, P], BF16)
+        nc.vector.memset(bias_rows[:], 0.0)
+        nc.sync.dma_start(
+            out=bias_rows[0 : 2 * 3 * UNIT_TILES, :], in_=bias.rearrange("i (c p) -> (i c) p", p=P)
+        )
         load_third(H_SIDE, GATE_R)
         load_third(H_SIDE, GATE_C)
         load_third(X_SIDE, GATE_C)
         load_third(X_SIDE, GATE_Z)
         load_third(H_SIDE, GATE_Z)
 
-        bias_rows = keep.tile([P, P], BF16)
-        nc.vector.memset(bias_rows[:], 0.0)
-        nc.scalar.dma_start(
-            out=bias_rows[0 : 2 * 3 * UNIT_TILES, :], in_=bias.rearrange("i (c p) -> (i c) p", p=P)
-        )
         ident_bf = keep.tile([P, P], BF16)
         make_identity(nc, ident_bf[:])
         ident_f32 = keep.tile([P, P], F32)

@@ -16,11 +16,11 @@ PACK = 4
 B = 128
 U = 512
 UNIT_TILES = U // P
-HALF = U // 2
-HALF_TILES = UNIT_TILES // 2
 
-X_SIDE, H_SIDE = 0, 1
+X, H = 0, 1
 GATE_Z, GATE_R, GATE_C = 0, 1, 2
+BIAS_ROWS = 8
+BIAS_CHUNKS = 2 * 3 * U // BIAS_ROWS // P
 
 FLOPS = 2 * 2 * B * U * 3 * U
 
@@ -36,200 +36,223 @@ def tile_gruskipcell_s_kernel(tc, inputs, h_tm1, kernel, recurrent_kernel, bias,
 
         raw = {}
         grouped = {}
+        for side in (X, H):
+            for gate in (GATE_R, GATE_C, GATE_Z):
+                raw[(side, gate)] = keep.tile([P, PACK, U], BF16, name="raw_%d_%d" % (side, gate))
+                grouped[(side, gate)] = keep.tile(
+                    [P, U, PACK], BF16, align_bytes=64, name="grouped_%d_%d" % (side, gate)
+                )
         w_codes = keep.tile([P, 2, 3 * U], U32, align_bytes=64)
         w_scales = keep.tile([P, 2, 3 * U], U8, align_bytes=64)
         act_grouped = keep.tile([P, 2, B, PACK], BF16, align_bytes=64)
         act_codes = keep.tile([P, 2, B], U32, align_bytes=64)
         act_scales = keep.tile([P, 2, B], U8, align_bytes=64)
 
-        def load_third(side, gate):
-            raw[(side, gate)] = keep.tile([P, PACK, U], BF16, name="raw_%d_%d" % (side, gate))
+        def load(side, gate, lo=0, hi=U):
             nc.sync.dma_start(
-                out=raw[(side, gate)][:],
-                in_=weights[side][:, gate * U : (gate + 1) * U].rearrange("(t p) n -> p t n", p=P),
+                out=raw[(side, gate)][:, :, lo:hi],
+                in_=weights[side][:, gate * U + lo : gate * U + hi].rearrange("(p t) n -> p t n", t=PACK),
             )
 
-        def regroup_third(side, gate):
-            grouped[(side, gate)] = keep.tile(
-                [P, U, PACK], BF16, align_bytes=64, name="grouped_%d_%d" % (side, gate)
+        def regroup(copy, side, gate, lo, hi):
+            copy(
+                out=grouped[(side, gate)][:, lo:hi, :].rearrange("p (c i) t -> p c t i", i=4),
+                in_=raw[(side, gate)][:, :, lo:hi].rearrange("p t (c i) -> p c t i", i=4),
             )
-            for half, copy in enumerate((nc.vector.tensor_copy, nc.scalar.copy)):
-                cols = slice(half * HALF, (half + 1) * HALF)
-                copy(
-                    out=grouped[(side, gate)][:, cols, :].rearrange("p (c i) t -> p c t i", i=4),
-                    in_=raw[(side, gate)][:, :, cols].rearrange("p t (c i) -> p c t i", i=4),
-                )
 
-        def quantise_third(side, gate):
-            for half in range(2):
-                cols = slice(half * HALF, (half + 1) * HALF)
-                w_cols = slice(gate * U + half * HALF, gate * U + (half + 1) * HALF)
-                nc.vector.quantize_mx(
-                    out=w_codes[:, side, w_cols].bitcast(FP8X4),
-                    scales=w_scales[:, side, w_cols],
-                    in_=grouped[(side, gate)][:, cols, :].rearrange("p c t -> p (c t)"),
-                )
+        def vector_regroup(side, gate, lo, hi):
+            regroup(nc.vector.tensor_copy, side, gate, lo, hi)
 
-        def products(sides, gate, name):
-            acc = []
-            for half in range(2):
-                acc.append(psum.tile([P, HALF_TILES, B], F32, tag="bank", name="%s_%d" % (name, half)))
-                for i in range(HALF_TILES):
-                    first = gate * U + half * HALF + i * P
-                    for side in sides:
-                        nc.tensor.matmul_mx(
-                            out=acc[half][:, i, :],
-                            lhsT=w_codes[:, side, first : first + P].bitcast(FP8X4),
-                            lhsT_scale=w_scales[:, side, first : first + P],
-                            rhs=act_codes[:, side, :].bitcast(FP8X4),
-                            rhs_scale=act_scales[:, side, :],
-                            start=(side == sides[0]),
-                            stop=(side == sides[-1]),
-                        )
+        def scalar_regroup(side, gate, lo, hi):
+            regroup(nc.scalar.copy, side, gate, lo, hi)
+
+        def quantise(side, gate, lo, hi):
+            w_cols = slice(gate * U + lo, gate * U + hi)
+            nc.vector.quantize_mx(
+                out=w_codes[:, side, w_cols].bitcast(FP8X4),
+                scales=w_scales[:, side, w_cols],
+                in_=grouped[(side, gate)][:, lo:hi, :].rearrange("p c t -> p (c t)"),
+            )
+
+        def product(side, gate, name):
+            acc = psum.tile([P, UNIT_TILES, B], F32, tag="bank", name=name)
+            for ut in range(UNIT_TILES):
+                first = gate * U + ut * P
+                nc.tensor.matmul_mx(
+                    out=acc[:, ut, :],
+                    lhsT=w_codes[:, side, first : first + P].bitcast(FP8X4),
+                    lhsT_scale=w_scales[:, side, first : first + P],
+                    rhs=act_codes[:, side, :].bitcast(FP8X4),
+                    rhs_scale=act_scales[:, side, :],
+                    start=True,
+                    stop=True,
+                )
             return acc
 
-        def scalar_function(dst, src_halves, func, bias_columns, scale):
-            for ut in range(UNIT_TILES):
-                nc.scalar.activation(
-                    out=dst[:, ut, :],
-                    in_=src_halves[ut // HALF_TILES][:, ut % HALF_TILES, :],
-                    func=func,
-                    bias=bias_columns[:, ut : ut + 1],
-                    scale=scale,
+        def unit_banks(name):
+            return [psum.tile([P, B], F32, tag="bank", name="%s_%d" % (name, ut)) for ut in range(UNIT_TILES)]
+
+        def gate_pass(acc, side, gate, lo, hi):
+            for ut in range(lo // P, hi // P):
+                first = gate * U + ut * P
+                nc.tensor.matmul_mx(
+                    out=acc[ut][:],
+                    lhsT=w_codes[:, side, first : first + P].bitcast(FP8X4),
+                    lhsT_scale=w_scales[:, side, first : first + P],
+                    rhs=act_codes[:, side, :].bitcast(FP8X4),
+                    rhs_scale=act_scales[:, side, :],
+                    start=(side == X),
+                    stop=(side == H),
                 )
 
-        def batch_rows(src, name):
-            rows = []
-            for half in range(2):
-                rows.append(psum.tile([B, HALF], F32, tag="bank", name="%s_%d" % (name, half)))
-                for i in range(HALF_TILES):
-                    nc.tensor.transpose(
-                        rows[half][:, i * P : (i + 1) * P], src[:, half * HALF_TILES + i, :], ident_f32[:]
-                    )
-            return rows
+        def scalar_function(dst, src, lo, hi, func, bias_columns, scale):
+            for ut in range(lo // P, hi // P):
+                nc.scalar.activation(
+                    out=dst[:, ut, :], in_=src[ut], func=func, bias=bias_columns[:, ut : ut + 1], scale=scale
+                )
 
-        def halves(tile):
-            return [tile[:, half * HALF_TILES : (half + 1) * HALF_TILES, :] for half in range(2)]
+        def by_unit(tile):
+            return [tile[:, ut, :] for ut in range(UNIT_TILES)]
+
+        def batch_rows(src, lo, hi, name):
+            rows = psum.tile([B, hi - lo], F32, tag="bank", name="%s_%d" % (name, lo))
+            for i in range((hi - lo) // P):
+                nc.tensor.transpose(rows[:, i * P : (i + 1) * P], src[:, lo // P + i, :], ident_f32[:])
+            return rows
 
         x_sb = keep.tile([B, U], BF16)
         h_sb = keep.tile([B, U], BF16)
-        load_third(X_SIDE, GATE_R)
-        nc.sync.dma_start(out=x_sb[:], in_=inputs)
-        nc.sync.dma_start(out=h_sb[:], in_=h_tm1)
-        bias_rows = keep.tile([P, P], BF16)
-        nc.vector.memset(bias_rows[:], 0.0)
-        nc.sync.dma_start(
-            out=bias_rows[0 : 2 * 3 * UNIT_TILES, :], in_=bias.rearrange("i (c p) -> (i c) p", p=P)
-        )
-        load_third(H_SIDE, GATE_R)
-        load_third(H_SIDE, GATE_C)
-        load_third(X_SIDE, GATE_C)
-        load_third(X_SIDE, GATE_Z)
-        load_third(H_SIDE, GATE_Z)
-
-        ident_bf = keep.tile([P, P], BF16)
-        make_identity(nc, ident_bf[:])
-        ident_f32 = keep.tile([P, P], F32)
-        make_identity(nc, ident_f32[:])
-
+        bias_rows = keep.tile([P, BIAS_CHUNKS, P], BF16)
         warm_in = keep.tile([P, 1], F32)
         warm_out = keep.tile([P, 1], F32)
         nc.vector.memset(warm_in[:], 0.0)
         nc.scalar.activation(out=warm_out[:], in_=warm_in[:], func=ACT.Tanh)
+        nc.vector.memset(bias_rows[:], 0.0)
+        load(X, GATE_R, 0, 256)
+        nc.sync.dma_start(out=x_sb[:], in_=inputs)
+        nc.sync.dma_start(out=h_sb[:], in_=h_tm1)
+        nc.sync.dma_start(
+            out=bias_rows[0:BIAS_ROWS, :, :].rearrange("r c p -> r (c p)"),
+            in_=bias.rearrange("i (r f) -> (i r) f", f=BIAS_CHUNKS * P),
+        )
+        load(X, GATE_R, 256, 512)
+        load(H, GATE_R)
+        load(H, GATE_C)
+        load(X, GATE_C)
+        load(X, GATE_Z)
+        load(H, GATE_Z, 0, 256)
+        load(H, GATE_Z, 256, 512)
 
-        regroup_third(X_SIDE, GATE_R)
+        ident_f32 = keep.tile([P, P], F32)
+        make_identity(nc, ident_f32[:])
+        ident_bf = keep.tile([P, P], BF16)
+        make_identity(nc, ident_bf[:])
 
-        x_t = psum.tile([P, PACK, B], BF16, tag="bank")
-        h_t = psum.tile([P, PACK, B], BF16, tag="bank")
-        bias_t = psum.tile([P, P], BF16, tag="bank")
-        for t in range(PACK):
-            nc.tensor.transpose(x_t[:, t, :], x_sb[:, t * P : (t + 1) * P], ident_bf[:])
-        for t in range(PACK):
-            nc.tensor.transpose(h_t[:, t, :], h_sb[:, t * P : (t + 1) * P], ident_bf[:])
-        nc.tensor.transpose(bias_t[:], bias_rows[:], ident_bf[:])
-        nc.vector.tensor_copy(out=act_grouped[:, X_SIDE, :, :], in_=x_t[:].rearrange("p t b -> p b t"))
-        nc.scalar.copy(out=act_grouped[:, H_SIDE, :, :], in_=h_t[:].rearrange("p t b -> p b t"))
+        x_t = psum.tile([P, 2, B], F32, tag="bank")
+        h_t = psum.tile([P, 2, B], F32, tag="bank")
+        bias_t = psum.tile([P, BIAS_CHUNKS, P], BF16, tag="bank")
+        for words_t, rows in ((x_t, x_sb), (h_t, h_sb)):
+            for u in range(2):
+                nc.tensor.transpose(words_t[:, u, :], rows[:].bitcast(F32)[:, u : U // 2 : 2], ident_f32[:])
+        for c in range(BIAS_CHUNKS):
+            nc.tensor.transpose(bias_t[:, c, :], bias_rows[:, c, :], ident_bf[:])
 
-        regroup_third(H_SIDE, GATE_R)
+        vector_regroup(X, GATE_R, 128, 256)
+        scalar_regroup(X, GATE_R, 0, 128)
+        for side, words_t in ((X, x_t), (H, h_t)):
+            nc.scalar.copy(
+                out=act_grouped[:, side, :, :].rearrange("p b t -> p (b t)").bitcast(F32),
+                in_=words_t[:].rearrange("p u b -> p b u"),
+            )
+        bias_cols = keep.tile([P, 2 * 3 * UNIT_TILES], F32)
+        nc.scalar.copy(
+            out=bias_cols[:].rearrange("p (r c) -> p r c", c=BIAS_CHUNKS),
+            in_=bias_t[:, :, 0:BIAS_ROWS].rearrange("p c r -> p r c"),
+        )
+        quantise(X, GATE_R, 0, 256)
+        vector_regroup(X, GATE_R, 256, 512)
         nc.vector.quantize_mx(
             out=act_codes[:].rearrange("p s b -> p (s b)").bitcast(FP8X4),
             scales=act_scales[:].rearrange("p s b -> p (s b)"),
             in_=act_grouped[:].rearrange("p s b t -> p (s b t)"),
         )
-        quantise_third(X_SIDE, GATE_R)
-
-        bias_cols = keep.tile([P, 2 * 3 * UNIT_TILES], F32)
-        nc.vector.tensor_copy(out=bias_cols[:], in_=bias_t[:, 0 : 2 * 3 * UNIT_TILES])
+        quantise(X, GATE_R, 256, 512)
+        both = keep.tile([P, 2 * UNIT_TILES], F32)
         gate_shift = keep.tile([P, 2 * UNIT_TILES], F32)
-        nc.vector.scalar_tensor_tensor(
-            out=gate_shift[:],
-            in0=bias_cols[:, 0 : 2 * UNIT_TILES],
-            scalar=2.5,
-            in1=bias_cols[:, 3 * UNIT_TILES : 5 * UNIT_TILES],
-            op0=ALU.add,
-            op1=ALU.add,
-        )
         rec_cand_bias = keep.tile([P, UNIT_TILES], F32)
-        nc.vector.tensor_scalar_mul(
-            out=rec_cand_bias[:], in0=bias_cols[:, 5 * UNIT_TILES : 6 * UNIT_TILES], scalar1=0.2
+        nc.gpsimd.tensor_tensor(
+            out=both[:], in0=bias_cols[:, 0 : 2 * UNIT_TILES],
+            in1=bias_cols[:, 3 * UNIT_TILES : 5 * UNIT_TILES], op=ALU.add,
         )
+        nc.gpsimd.tensor_scalar(
+            out=gate_shift[:], in0=both[:], scalar1=1.0, scalar2=2.5, op0=ALU.mult, op1=ALU.add
+        )
+        nc.gpsimd.tensor_scalar(
+            out=rec_cand_bias[:], in0=bias_cols[:, 5 * UNIT_TILES : 6 * UNIT_TILES],
+            scalar1=0.2, scalar2=0.0, op0=ALU.mult, op1=ALU.add,
+        )
+        z_shift = gate_shift[:, 0:UNIT_TILES]
+        r_shift = gate_shift[:, UNIT_TILES : 2 * UNIT_TILES]
+        cand_bias = bias_cols[:, 2 * UNIT_TILES : 3 * UNIT_TILES]
 
-        regroup_third(H_SIDE, GATE_C)
-        quantise_third(H_SIDE, GATE_R)
-        acc_r = products((X_SIDE, H_SIDE), GATE_R, "acc_r")
-        regroup_third(X_SIDE, GATE_C)
-        quantise_third(H_SIDE, GATE_C)
-        acc_rec = products((H_SIDE,), GATE_C, "acc_rec")
+        acc_r = unit_banks("acc_r")
+        gate_pass(acc_r, X, GATE_R, 0, U)
+        vector_regroup(H, GATE_R, 0, 256)
+        scalar_regroup(H, GATE_R, 256, 512)
+        vector_regroup(H, GATE_C, 0, 256)
+        scalar_regroup(H, GATE_C, 256, 512)
+        quantise(H, GATE_R, 0, 512)
+        gate_pass(acc_r, H, GATE_R, 0, U)
+        vector_regroup(X, GATE_C, 0, 256)
+        scalar_regroup(X, GATE_C, 256, 512)
+        quantise(H, GATE_C, 0, 512)
+        acc_rec = product(H, GATE_C, "acc_rec")
 
         r5 = keep.tile([P, UNIT_TILES, B], F32)
-        scalar_function(r5, acc_r, ACT.Relu, gate_shift[:, UNIT_TILES : 2 * UNIT_TILES], 1.0)
+        scalar_function(r5, [acc[:] for acc in acc_r], 0, U, ACT.Relu, r_shift, 1.0)
         rec_fifth = keep.tile([P, UNIT_TILES, B], F32)
-        scalar_function(rec_fifth, acc_rec, ACT.Identity, rec_cand_bias, 0.2)
+        scalar_function(rec_fifth, by_unit(acc_rec), 0, U, ACT.Identity, rec_cand_bias, 0.2)
 
-        regroup_third(X_SIDE, GATE_Z)
-        quantise_third(X_SIDE, GATE_C)
-        acc_x = products((X_SIDE,), GATE_C, "acc_x")
-        regroup_third(H_SIDE, GATE_Z)
+        vector_regroup(X, GATE_Z, 0, 256)
+        scalar_regroup(X, GATE_Z, 256, 512)
+        quantise(X, GATE_C, 0, 512)
+        acc_x = product(X, GATE_C, "acc_x")
+        vector_regroup(H, GATE_Z, 128, 256)
+        scalar_regroup(H, GATE_Z, 0, 128)
 
         gated = keep.tile([P, UNIT_TILES, B], F32)
-        for half in range(2):
-            nc.vector.scalar_tensor_tensor(
-                out=halves(gated)[half], in0=halves(r5)[half], scalar=5.0, in1=halves(rec_fifth)[half],
-                op0=ALU.min, op1=ALU.mult,
-            )
+        nc.vector.scalar_tensor_tensor(
+            out=gated[:], in0=r5[:], scalar=5.0, in1=rec_fifth[:], op0=ALU.min, op1=ALU.mult
+        )
         pre = keep.tile([P, UNIT_TILES, B], F32)
-        for half in range(2):
-            nc.vector.tensor_tensor(
-                out=halves(pre)[half], in0=acc_x[half][:], in1=halves(gated)[half], op=ALU.add
-            )
-
-        quantise_third(X_SIDE, GATE_Z)
-        quantise_third(H_SIDE, GATE_Z)
-        acc_z = products((X_SIDE, H_SIDE), GATE_Z, "acc_z")
-
+        nc.vector.tensor_tensor(out=pre[:], in0=acc_x[:], in1=gated[:], op=ALU.add)
         hh = keep.tile([P, UNIT_TILES, B], F32)
-        scalar_function(hh, halves(pre), ACT.Tanh, bias_cols[:, 2 * UNIT_TILES : 3 * UNIT_TILES], 1.0)
-        z5 = keep.tile([P, UNIT_TILES, B], F32)
-        scalar_function(z5, acc_z, ACT.Relu, gate_shift[:, 0:UNIT_TILES], 1.0)
+        scalar_function(hh, by_unit(pre), 0, U, ACT.Tanh, cand_bias, 1.0)
 
-        hh_rows = batch_rows(hh, "hh_rows")
+        quantise(X, GATE_Z, 0, 512)
+        acc_z = unit_banks("acc_z")
+        gate_pass(acc_z, X, GATE_Z, 0, U)
+        quantise(H, GATE_Z, 0, 256)
+        gate_pass(acc_z, H, GATE_Z, 0, 256)
+        hh_rows = batch_rows(hh, 0, U, "hh_rows")
+        vector_regroup(H, GATE_Z, 256, 512)
+        quantise(H, GATE_Z, 256, 512)
+        gate_pass(acc_z, H, GATE_Z, 256, 512)
         diff = keep.tile([B, U], F32)
-        for half in range(2):
-            cols = slice(half * HALF, (half + 1) * HALF)
-            nc.vector.tensor_tensor(
-                out=diff[:, cols], in0=h_sb[:, cols], in1=hh_rows[half][:], op=ALU.subtract
-            )
-        z5_rows = batch_rows(z5, "z5_rows")
+        nc.vector.tensor_tensor(out=diff[:], in0=h_sb[:], in1=hh_rows[:], op=ALU.subtract)
+
+        z5 = keep.tile([P, UNIT_TILES, B], F32)
         moved = keep.tile([B, U], F32)
         out_sb = keep.tile([B, U], F32)
-        for half in range(2):
-            cols = slice(half * HALF, (half + 1) * HALF)
+        for lo, hi in ((0, 256), (256, 512)):
+            scalar_function(z5, [acc[:] for acc in acc_z], lo, hi, ACT.Relu, z_shift, 1.0)
+            z5_rows = batch_rows(z5, lo, hi, "z5_rows")
             nc.vector.scalar_tensor_tensor(
-                out=moved[:, cols], in0=z5_rows[half][:], scalar=5.0, in1=diff[:, cols],
+                out=moved[:, lo:hi], in0=z5_rows[:], scalar=5.0, in1=diff[:, lo:hi],
                 op0=ALU.min, op1=ALU.mult,
             )
             nc.vector.scalar_tensor_tensor(
-                out=out_sb[:, cols], in0=moved[:, cols], scalar=0.2, in1=hh_rows[half][:],
+                out=out_sb[:, lo:hi], in0=moved[:, lo:hi], scalar=0.2, in1=hh_rows[:, lo:hi],
                 op0=ALU.mult, op1=ALU.add,
             )
-            nc.sync.dma_start(out=out[:, cols], in_=out_sb[:, cols])
+            nc.sync.dma_start(out=out[:, lo:hi], in_=out_sb[:, lo:hi])

@@ -120,6 +120,8 @@ def tile_gruskipcell_s_kernel(tc, inputs, h_tm1, kernel, recurrent_kernel, bias,
                 nc.tensor.transpose(rows[:, i * P : (i + 1) * P], src[:, lo // P + i, :], ident_f32[:])
             return rows
 
+        HALVES = ((256, 512), (0, 256))
+
         x_sb = keep.tile([B, U], BF16)
         h_sb = keep.tile([B, U], BF16)
         bias_rows = keep.tile([P, BIAS_CHUNKS, P], BF16)
@@ -128,20 +130,18 @@ def tile_gruskipcell_s_kernel(tc, inputs, h_tm1, kernel, recurrent_kernel, bias,
         nc.vector.memset(warm_in[:], 0.0)
         nc.scalar.activation(out=warm_out[:], in_=warm_in[:], func=ACT.Tanh)
         nc.vector.memset(bias_rows[:], 0.0)
-        load(X, GATE_R, 0, 256)
+        load(X, GATE_R)
         nc.sync.dma_start(out=x_sb[:], in_=inputs)
         nc.sync.dma_start(out=h_sb[:], in_=h_tm1)
         nc.sync.dma_start(
             out=bias_rows[0:BIAS_ROWS, :, :].rearrange("r c p -> r (c p)"),
             in_=bias.rearrange("i (r f) -> (i r) f", f=BIAS_CHUNKS * P),
         )
-        load(X, GATE_R, 256, 512)
         load(H, GATE_R)
         load(H, GATE_C)
         load(X, GATE_C)
         load(X, GATE_Z)
-        load(H, GATE_Z, 0, 256)
-        load(H, GATE_Z, 256, 512)
+        load(H, GATE_Z)
 
         ident_f32 = keep.tile([P, P], F32)
         make_identity(nc, ident_f32[:])
@@ -157,8 +157,8 @@ def tile_gruskipcell_s_kernel(tc, inputs, h_tm1, kernel, recurrent_kernel, bias,
         for c in range(BIAS_CHUNKS):
             nc.tensor.transpose(bias_t[:, c, :], bias_rows[:, c, :], ident_bf[:])
 
-        vector_regroup(X, GATE_R, 128, 256)
-        scalar_regroup(X, GATE_R, 0, 128)
+        vector_regroup(X, GATE_R, 192, 512)
+        scalar_regroup(X, GATE_R, 0, 192)
         for side, words_t in ((X, x_t), (H, h_t)):
             nc.scalar.copy(
                 out=act_grouped[:, side, :, :].rearrange("p b t -> p (b t)").bitcast(F32),
@@ -169,14 +169,14 @@ def tile_gruskipcell_s_kernel(tc, inputs, h_tm1, kernel, recurrent_kernel, bias,
             out=bias_cols[:].rearrange("p (r c) -> p r c", c=BIAS_CHUNKS),
             in_=bias_t[:, :, 0:BIAS_ROWS].rearrange("p c r -> p r c"),
         )
-        quantise(X, GATE_R, 0, 256)
-        vector_regroup(X, GATE_R, 256, 512)
+        quantise(X, GATE_R, 0, 512)
+        vector_regroup(H, GATE_R, 0, 256)
+        scalar_regroup(H, GATE_R, 256, 512)
         nc.vector.quantize_mx(
             out=act_codes[:].rearrange("p s b -> p (s b)").bitcast(FP8X4),
             scales=act_scales[:].rearrange("p s b -> p (s b)"),
             in_=act_grouped[:].rearrange("p s b t -> p (s b t)"),
         )
-        quantise(X, GATE_R, 256, 512)
         both = keep.tile([P, 2 * UNIT_TILES], F32)
         gate_shift = keep.tile([P, 2 * UNIT_TILES], F32)
         rec_cand_bias = keep.tile([P, UNIT_TILES], F32)
@@ -197,8 +197,6 @@ def tile_gruskipcell_s_kernel(tc, inputs, h_tm1, kernel, recurrent_kernel, bias,
 
         acc_r = unit_banks("acc_r")
         gate_pass(acc_r, X, GATE_R, 0, U)
-        vector_regroup(H, GATE_R, 0, 256)
-        scalar_regroup(H, GATE_R, 256, 512)
         vector_regroup(H, GATE_C, 0, 256)
         scalar_regroup(H, GATE_C, 256, 512)
         quantise(H, GATE_R, 0, 512)
@@ -207,52 +205,62 @@ def tile_gruskipcell_s_kernel(tc, inputs, h_tm1, kernel, recurrent_kernel, bias,
         scalar_regroup(X, GATE_C, 256, 512)
         quantise(H, GATE_C, 0, 512)
         acc_rec = product(H, GATE_C, "acc_rec")
+        vector_regroup(X, GATE_Z, 256, 512)
+        scalar_regroup(X, GATE_Z, 0, 256)
+        quantise(X, GATE_C, 0, 512)
+        acc_x = product(X, GATE_C, "acc_x")
 
         r5 = keep.tile([P, UNIT_TILES, B], F32)
         scalar_function(r5, [acc[:] for acc in acc_r], 0, U, ACT.Relu, r_shift, 1.0)
         rec_fifth = keep.tile([P, UNIT_TILES, B], F32)
         scalar_function(rec_fifth, by_unit(acc_rec), 0, U, ACT.Identity, rec_cand_bias, 0.2)
 
-        vector_regroup(X, GATE_Z, 0, 256)
-        scalar_regroup(X, GATE_Z, 256, 512)
-        quantise(X, GATE_C, 0, 512)
-        acc_x = product(X, GATE_C, "acc_x")
-        vector_regroup(H, GATE_Z, 128, 256)
-        scalar_regroup(H, GATE_Z, 0, 128)
+        vector_regroup(H, GATE_Z, 256, 512)
+        scalar_regroup(H, GATE_Z, 0, 256)
+        quantise(X, GATE_Z, 0, 512)
+        quantise(H, GATE_Z, 256, 512)
+        acc_z = unit_banks("acc_z")
+        for lo, hi in HALVES:
+            gate_pass(acc_z, X, GATE_Z, lo, hi)
+            if lo:
+                gate_pass(acc_z, H, GATE_Z, lo, hi)
 
         gated = keep.tile([P, UNIT_TILES, B], F32)
-        nc.vector.scalar_tensor_tensor(
-            out=gated[:], in0=r5[:], scalar=5.0, in1=rec_fifth[:], op0=ALU.min, op1=ALU.mult
-        )
         pre = keep.tile([P, UNIT_TILES, B], F32)
-        nc.vector.tensor_tensor(out=pre[:], in0=acc_x[:], in1=gated[:], op=ALU.add)
-        hh = keep.tile([P, UNIT_TILES, B], F32)
-        scalar_function(hh, by_unit(pre), 0, U, ACT.Tanh, cand_bias, 1.0)
-
-        quantise(X, GATE_Z, 0, 512)
-        acc_z = unit_banks("acc_z")
-        gate_pass(acc_z, X, GATE_Z, 0, U)
-        quantise(H, GATE_Z, 0, 256)
-        gate_pass(acc_z, H, GATE_Z, 0, 256)
-        hh_rows = batch_rows(hh, 0, U, "hh_rows")
-        vector_regroup(H, GATE_Z, 256, 512)
-        quantise(H, GATE_Z, 256, 512)
-        gate_pass(acc_z, H, GATE_Z, 256, 512)
-        diff = keep.tile([B, U], F32)
-        nc.vector.tensor_tensor(out=diff[:], in0=h_sb[:], in1=hh_rows[:], op=ALU.subtract)
-
-        z5 = keep.tile([P, UNIT_TILES, B], F32)
-        moved = keep.tile([B, U], F32)
-        out_sb = keep.tile([B, U], F32)
-        for lo, hi in ((0, 256), (256, 512)):
-            scalar_function(z5, [acc[:] for acc in acc_z], lo, hi, ACT.Relu, z_shift, 1.0)
-            z5_rows = batch_rows(z5, lo, hi, "z5_rows")
+        for lo, hi in HALVES:
+            uts = slice(lo // P, hi // P)
             nc.vector.scalar_tensor_tensor(
-                out=moved[:, lo:hi], in0=z5_rows[:], scalar=5.0, in1=diff[:, lo:hi],
+                out=gated[:, uts, :], in0=r5[:, uts, :], scalar=5.0, in1=rec_fifth[:, uts, :],
                 op0=ALU.min, op1=ALU.mult,
             )
+        for lo, hi in HALVES:
+            uts = slice(lo // P, hi // P)
+            nc.vector.tensor_tensor(
+                out=pre[:, uts, :], in0=acc_x[:, uts, :], in1=gated[:, uts, :], op=ALU.add
+            )
+        quantise(H, GATE_Z, 0, 256)
+        gate_pass(acc_z, H, GATE_Z, 0, 256)
+
+        hh = keep.tile([P, UNIT_TILES, B], F32)
+        z5 = keep.tile([P, UNIT_TILES, B], F32)
+        diff = keep.tile([B, U], F32)
+        moved = keep.tile([B, U], F32)
+        out_sb = keep.tile([B, U], F32)
+        banks_z = [acc[:] for acc in acc_z]
+        scalar_function(z5, banks_z, 256, 512, ACT.Relu, z_shift, 1.0)
+        scalar_function(hh, by_unit(pre), 256, 512, ACT.Tanh, cand_bias, 1.0)
+        scalar_function(hh, by_unit(pre), 0, 256, ACT.Tanh, cand_bias, 1.0)
+        scalar_function(z5, banks_z, 0, 256, ACT.Relu, z_shift, 1.0)
+        hh_rows = [batch_rows(hh, lo, hi, "hh_rows") for lo, hi in HALVES]
+        z5_rows = [batch_rows(z5, lo, hi, "z5_rows") for lo, hi in HALVES]
+        for rows, (lo, hi) in zip(hh_rows, HALVES):
+            nc.vector.tensor_tensor(out=diff[:, lo:hi], in0=h_sb[:, lo:hi], in1=rows[:], op=ALU.subtract)
+        for rows, (lo, hi) in zip(z5_rows, HALVES):
             nc.vector.scalar_tensor_tensor(
-                out=out_sb[:, lo:hi], in0=moved[:, lo:hi], scalar=0.2, in1=hh_rows[:, lo:hi],
-                op0=ALU.mult, op1=ALU.add,
+                out=moved[:, lo:hi], in0=rows[:], scalar=5.0, in1=diff[:, lo:hi], op0=ALU.min, op1=ALU.mult
+            )
+        for rows, (lo, hi) in zip(hh_rows, HALVES):
+            nc.vector.scalar_tensor_tensor(
+                out=out_sb[:, lo:hi], in0=moved[:, lo:hi], scalar=0.2, in1=rows[:], op0=ALU.mult, op1=ALU.add
             )
             nc.sync.dma_start(out=out[:, lo:hi], in_=out_sb[:, lo:hi])

@@ -31,7 +31,8 @@ def tile_gruskipcell_s_kernel(tc, inputs, h_tm1, kernel, recurrent_kernel, bias,
 
     with ExitStack() as ctx:
         keep = ctx.enter_context(tc.tile_pool(name="keep", bufs=1))
-        psum = ctx.enter_context(tc.psum_pool(name="psum", bufs=8))
+        psum = ctx.enter_context(tc.psum_pool(name="psum", bufs=7))
+        idle_psum = ctx.enter_context(tc.psum_pool(name="idle_psum", bufs=1))
         ctx.enter_context(tc.manual_schedule())
 
         raw = {}
@@ -104,6 +105,20 @@ def tile_gruskipcell_s_kernel(tc, inputs, h_tm1, kernel, recurrent_kernel, bias,
                     start=(side == X),
                     stop=(side == H),
                 )
+
+        idle_acc = idle_psum.tile([B, U], F32)
+
+        def keep_busy():
+            third = slice(GATE_R * U, (GATE_R + 1) * U)
+            nc.tensor.matmul_mx(
+                out=idle_acc[:],
+                lhsT=act_codes[:, X, :].bitcast(FP8X4),
+                lhsT_scale=act_scales[:, X, :],
+                rhs=w_codes[:, X, third].bitcast(FP8X4),
+                rhs_scale=w_scales[:, X, third],
+                start=True,
+                stop=True,
+            )
 
         def scalar_function(dst, src, lo, hi, func, bias_columns, scale):
             for ut in range(lo // P, hi // P):
@@ -197,18 +212,23 @@ def tile_gruskipcell_s_kernel(tc, inputs, h_tm1, kernel, recurrent_kernel, bias,
 
         acc_r = unit_banks("acc_r")
         gate_pass(acc_r, X, GATE_R, 0, U)
+        keep_busy()
+        keep_busy()
         vector_regroup(H, GATE_C, 0, 256)
         scalar_regroup(H, GATE_C, 256, 512)
         quantise(H, GATE_R, 0, 512)
         gate_pass(acc_r, H, GATE_R, 0, U)
+        keep_busy()
         vector_regroup(X, GATE_C, 0, 256)
         scalar_regroup(X, GATE_C, 256, 512)
         quantise(H, GATE_C, 0, 512)
         acc_rec = product(H, GATE_C, "acc_rec")
+        keep_busy()
         vector_regroup(X, GATE_Z, 256, 512)
         scalar_regroup(X, GATE_Z, 0, 256)
         quantise(X, GATE_C, 0, 512)
         acc_x = product(X, GATE_C, "acc_x")
+        keep_busy()
 
         r5 = keep.tile([P, UNIT_TILES, B], F32)
         scalar_function(r5, [acc[:] for acc in acc_r], 0, U, ACT.Relu, r_shift, 1.0)
@@ -239,6 +259,7 @@ def tile_gruskipcell_s_kernel(tc, inputs, h_tm1, kernel, recurrent_kernel, bias,
                 out=pre[:, uts, :], in0=acc_x[:, uts, :], in1=gated[:, uts, :], op=ALU.add
             )
         quantise(H, GATE_Z, 0, 256)
+        keep_busy()
         gate_pass(acc_z, H, GATE_Z, 0, 256)
 
         hh = keep.tile([P, UNIT_TILES, B], F32)

@@ -192,19 +192,18 @@ def tile_gruskipcell_s_kernel(tc, inputs, h_tm1, kernel, recurrent_kernel, bias,
             scales=act_scales[:].rearrange("p s b -> p (s b)"),
             in_=act_grouped[:].rearrange("p s b t -> p (s b t)"),
         )
-        both = keep.tile([P, 2 * UNIT_TILES], F32)
         gate_shift = keep.tile([P, 2 * UNIT_TILES], F32)
+        nc.vector.scalar_tensor_tensor(
+            out=gate_shift[:],
+            in0=bias_cols[:, 0 : 2 * UNIT_TILES],
+            scalar=2.5,
+            in1=bias_cols[:, 3 * UNIT_TILES : 5 * UNIT_TILES],
+            op0=ALU.add,
+            op1=ALU.add,
+        )
         rec_cand_bias = keep.tile([P, UNIT_TILES], F32)
-        nc.gpsimd.tensor_tensor(
-            out=both[:], in0=bias_cols[:, 0 : 2 * UNIT_TILES],
-            in1=bias_cols[:, 3 * UNIT_TILES : 5 * UNIT_TILES], op=ALU.add,
-        )
-        nc.gpsimd.tensor_scalar(
-            out=gate_shift[:], in0=both[:], scalar1=1.0, scalar2=2.5, op0=ALU.mult, op1=ALU.add
-        )
-        nc.gpsimd.tensor_scalar(
-            out=rec_cand_bias[:], in0=bias_cols[:, 5 * UNIT_TILES : 6 * UNIT_TILES],
-            scalar1=0.2, scalar2=0.0, op0=ALU.mult, op1=ALU.add,
+        nc.vector.tensor_scalar_mul(
+            out=rec_cand_bias[:], in0=bias_cols[:, 5 * UNIT_TILES : 6 * UNIT_TILES], scalar1=0.2
         )
         z_shift = gate_shift[:, 0:UNIT_TILES]
         r_shift = gate_shift[:, UNIT_TILES : 2 * UNIT_TILES]

@@ -19,6 +19,7 @@ UNIT_TILES = U // P
 
 X, H = 0, 1
 GATE_Z, GATE_R, GATE_C = 0, 1, 2
+RUN = 8
 BIAS_ROWS = 8
 BIAS_CHUNKS = 2 * 3 * U // BIAS_ROWS // P
 
@@ -57,8 +58,8 @@ def tile_gruskipcell_s_kernel(tc, inputs, h_tm1, kernel, recurrent_kernel, bias,
 
         def regroup(copy, side, gate, lo, hi):
             copy(
-                out=grouped[(side, gate)][:, lo:hi, :].rearrange("p (c i) t -> p c t i", i=4),
-                in_=raw[(side, gate)][:, :, lo:hi].rearrange("p t (c i) -> p c t i", i=4),
+                out=grouped[(side, gate)][:, lo:hi, :].rearrange("p (c i) t -> p c t i", i=RUN),
+                in_=raw[(side, gate)][:, :, lo:hi].rearrange("p t (c i) -> p c t i", i=RUN),
             )
 
         def vector_regroup(side, gate, lo, hi):

@@ -173,8 +173,8 @@ def tile_gruskipcell_s_kernel(tc, inputs, h_tm1, kernel, recurrent_kernel, bias,
         for c in range(BIAS_CHUNKS):
             nc.tensor.transpose(bias_t[:, c, :], bias_rows[:, c, :], ident_bf[:])
 
-        vector_regroup(X, GATE_R, 192, 512)
-        scalar_regroup(X, GATE_R, 0, 192)
+        vector_regroup(X, GATE_R, 0, 256)
+        vector_regroup(X, GATE_R, 256, 512)
         for side, words_t in ((X, x_t), (H, h_t)):
             nc.scalar.copy(
                 out=act_grouped[:, side, :, :].rearrange("p b t -> p (b t)").bitcast(F32),
@@ -185,7 +185,8 @@ def tile_gruskipcell_s_kernel(tc, inputs, h_tm1, kernel, recurrent_kernel, bias,
             out=bias_cols[:].rearrange("p (r c) -> p r c", c=BIAS_CHUNKS),
             in_=bias_t[:, :, 0:BIAS_ROWS].rearrange("p c r -> p r c"),
         )
-        quantise(X, GATE_R, 0, 512)
+        quantise(X, GATE_R, 0, 256)
+        quantise(X, GATE_R, 256, 512)
         vector_regroup(H, GATE_R, 0, 256)
         scalar_regroup(H, GATE_R, 256, 512)
         nc.vector.quantize_mx(
@@ -219,31 +220,31 @@ def tile_gruskipcell_s_kernel(tc, inputs, h_tm1, kernel, recurrent_kernel, bias,
         quantise(H, GATE_R, 0, 512)
         gate_pass(acc_r, H, GATE_R, 0, U)
         keep_busy()
-        vector_regroup(X, GATE_C, 0, 256)
-        scalar_regroup(X, GATE_C, 256, 512)
+
+        vector_regroup(X, GATE_C, 0, 320)
+        scalar_regroup(X, GATE_C, 320, 512)
+        r5 = keep.tile([P, UNIT_TILES, B], F32)
+        scalar_function(r5, [acc[:] for acc in acc_r], 0, U, ACT.Relu, r_shift, 1.0)
         quantise(H, GATE_C, 0, 512)
         acc_rec = product(H, GATE_C, "acc_rec")
         keep_busy()
-        vector_regroup(X, GATE_Z, 256, 512)
-        scalar_regroup(X, GATE_Z, 0, 256)
+
+        vector_regroup(X, GATE_Z, 192, 512)
+        scalar_regroup(X, GATE_Z, 0, 192)
+        rec_fifth = keep.tile([P, UNIT_TILES, B], F32)
+        scalar_function(rec_fifth, by_unit(acc_rec), 0, U, ACT.Identity, rec_cand_bias, 0.2)
         quantise(X, GATE_C, 0, 512)
         acc_x = product(X, GATE_C, "acc_x")
         keep_busy()
 
-        r5 = keep.tile([P, UNIT_TILES, B], F32)
-        scalar_function(r5, [acc[:] for acc in acc_r], 0, U, ACT.Relu, r_shift, 1.0)
-        rec_fifth = keep.tile([P, UNIT_TILES, B], F32)
-        scalar_function(rec_fifth, by_unit(acc_rec), 0, U, ACT.Identity, rec_cand_bias, 0.2)
-
-        vector_regroup(H, GATE_Z, 256, 512)
-        scalar_regroup(H, GATE_Z, 0, 256)
         quantise(X, GATE_Z, 0, 512)
-        quantise(H, GATE_Z, 256, 512)
         acc_z = unit_banks("acc_z")
         for lo, hi in HALVES:
             gate_pass(acc_z, X, GATE_Z, lo, hi)
-            if lo:
-                gate_pass(acc_z, H, GATE_Z, lo, hi)
+        keep_busy()
+        keep_busy()
+        scalar_regroup(H, GATE_Z, 256, 384)
+        scalar_regroup(H, GATE_Z, 0, 256)
 
         gated = keep.tile([P, UNIT_TILES, B], F32)
         pre = keep.tile([P, UNIT_TILES, B], F32)
@@ -253,27 +254,28 @@ def tile_gruskipcell_s_kernel(tc, inputs, h_tm1, kernel, recurrent_kernel, bias,
                 out=gated[:, uts, :], in0=r5[:, uts, :], scalar=5.0, in1=rec_fifth[:, uts, :],
                 op0=ALU.min, op1=ALU.mult,
             )
+        vector_regroup(H, GATE_Z, 384, 512)
         for lo, hi in HALVES:
             uts = slice(lo // P, hi // P)
             nc.vector.tensor_tensor(
                 out=pre[:, uts, :], in0=acc_x[:, uts, :], in1=gated[:, uts, :], op=ALU.add
             )
-        quantise(H, GATE_Z, 0, 256)
-        keep_busy()
-        gate_pass(acc_z, H, GATE_Z, 0, 256)
+            quantise(H, GATE_Z, lo, hi)
 
         hh = keep.tile([P, UNIT_TILES, B], F32)
         z5 = keep.tile([P, UNIT_TILES, B], F32)
         diff = keep.tile([B, U], F32)
         moved = keep.tile([B, U], F32)
         out_sb = keep.tile([B, U], F32)
-        banks_z = [acc[:] for acc in acc_z]
-        scalar_function(z5, banks_z, 256, 512, ACT.Relu, z_shift, 1.0)
-        scalar_function(hh, by_unit(pre), 256, 512, ACT.Tanh, cand_bias, 1.0)
-        scalar_function(hh, by_unit(pre), 0, 256, ACT.Tanh, cand_bias, 1.0)
-        scalar_function(z5, banks_z, 0, 256, ACT.Relu, z_shift, 1.0)
-        hh_rows = [batch_rows(hh, lo, hi, "hh_rows") for lo, hi in HALVES]
-        z5_rows = [batch_rows(z5, lo, hi, "z5_rows") for lo, hi in HALVES]
+        hh_rows = []
+        for lo, hi in HALVES:
+            scalar_function(hh, by_unit(pre), lo, hi, ACT.Tanh, cand_bias, 1.0)
+            gate_pass(acc_z, H, GATE_Z, lo, hi)
+            hh_rows.append(batch_rows(hh, lo, hi, "hh_rows"))
+        z5_rows = []
+        for lo, hi in HALVES:
+            scalar_function(z5, [acc[:] for acc in acc_z], lo, hi, ACT.Relu, z_shift, 1.0)
+            z5_rows.append(batch_rows(z5, lo, hi, "z5_rows"))
         for rows, (lo, hi) in zip(hh_rows, HALVES):
             nc.vector.tensor_tensor(out=diff[:, lo:hi], in0=h_sb[:, lo:hi], in1=rows[:], op=ALU.subtract)
         for rows, (lo, hi) in zip(z5_rows, HALVES):

from contextlib import ExitStack

import concourse.mybir as mybir
from concourse.masks import make_identity

BF16 = mybir.dt.bfloat16
F32 = mybir.dt.float32
U32 = mybir.dt.uint32
U8 = mybir.dt.uint8
FP8X4 = mybir.dt.float8_e4m3fn_x4
ALU = mybir.AluOpType
ACT = mybir.ActivationFunctionType

P = 128
PACK = 4
B = 128
U = 512
UNIT_TILES = U // P

X, H = 0, 1
GATE_Z, GATE_R, GATE_C = 0, 1, 2
RUN = 8
BIAS_ROWS = 8
BIAS_CHUNKS = 2 * 3 * U // BIAS_ROWS // P

FLOPS = 2 * 2 * B * U * 3 * U


def tile_gruskipcell_s_kernel(tc, inputs, h_tm1, kernel, recurrent_kernel, bias, out):
    nc = tc.nc
    weights = (kernel, recurrent_kernel)

    with ExitStack() as ctx:
        keep = ctx.enter_context(tc.tile_pool(name="keep", bufs=1))
        psum = ctx.enter_context(tc.psum_pool(name="psum", bufs=7))
        idle_psum = ctx.enter_context(tc.psum_pool(name="idle_psum", bufs=1))
        ctx.enter_context(tc.manual_schedule())

        raw = {}
        grouped = {}
        for side in (X, H):
            for gate in (GATE_R, GATE_C, GATE_Z):
                raw[(side, gate)] = keep.tile([P, PACK, U], BF16, name="raw_%d_%d" % (side, gate))
                grouped[(side, gate)] = keep.tile(
                    [P, U, PACK], BF16, align_bytes=64, name="grouped_%d_%d" % (side, gate)
                )
        w_codes = keep.tile([P, 2, 3 * U], U32, align_bytes=64)
        w_scales = keep.tile([P, 2, 3 * U], U8, align_bytes=64)
        act_grouped = keep.tile([P, 2, B, PACK], BF16, align_bytes=64)
        act_codes = keep.tile([P, 2, B], U32, align_bytes=64)
        act_scales = keep.tile([P, 2, B], U8, align_bytes=64)

        def load(side, gate, lo=0, hi=U):
            nc.sync.dma_start(
                out=raw[(side, gate)][:, :, lo:hi],
                in_=weights[side][:, gate * U + lo : gate * U + hi].rearrange("(p t) n -> p t n", t=PACK),
            )

        def regroup(copy, side, gate, lo, hi):
            copy(
                out=grouped[(side, gate)][:, lo:hi, :].rearrange("p (c i) t -> p c t i", i=RUN),
                in_=raw[(side, gate)][:, :, lo:hi].rearrange("p t (c i) -> p c t i", i=RUN),
            )

        def vector_regroup(side, gate, lo, hi):
            regroup(nc.vector.tensor_copy, side, gate, lo, hi)

        def scalar_regroup(side, gate, lo, hi):
            regroup(nc.scalar.copy, side, gate, lo, hi)

        def quantise(side, gate, lo, hi):
            w_cols = slice(gate * U + lo, gate * U + hi)
            nc.vector.quantize_mx(
                out=w_codes[:, side, w_cols].bitcast(FP8X4),
                scales=w_scales[:, side, w_cols],
                in_=grouped[(side, gate)][:, lo:hi, :].rearrange("p c t -> p (c t)"),
            )

        def product(side, gate, name):
            acc = psum.tile([P, UNIT_TILES, B], F32, tag="bank", name=name)
            for ut in range(UNIT_TILES):
                first = gate * U + ut * P
                nc.tensor.matmul_mx(
                    out=acc[:, ut, :],
                    lhsT=w_codes[:, side, first : first + P].bitcast(FP8X4),
                    lhsT_scale=w_scales[:, side, first : first + P],
                    rhs=act_codes[:, side, :].bitcast(FP8X4),
                    rhs_scale=act_scales[:, side, :],
                    start=True,
                    stop=True,
                )
            return acc

        def unit_banks(name):
            return [psum.tile([P, B], F32, tag="bank", name="%s_%d" % (name, ut)) for ut in range(UNIT_TILES)]

        def gate_pass(acc, side, gate, lo, hi):
            for ut in range(lo // P, hi // P):
                first = gate * U + ut * P
                nc.tensor.matmul_mx(
                    out=acc[ut][:],
                    lhsT=w_codes[:, side, first : first + P].bitcast(FP8X4),
                    lhsT_scale=w_scales[:, side, first : first + P],
                    rhs=act_codes[:, side, :].bitcast(FP8X4),
                    rhs_scale=act_scales[:, side, :],
                    start=(side == X),
                    stop=(side == H),
                )

        idle_acc = idle_psum.tile([B, U], F32)

        def keep_busy():
            third = slice(GATE_R * U, (GATE_R + 1) * U)
            nc.tensor.matmul_mx(
                out=idle_acc[:],
                lhsT=act_codes[:, X, :].bitcast(FP8X4),
                lhsT_scale=act_scales[:, X, :],
                rhs=w_codes[:, X, third].bitcast(FP8X4),
                rhs_scale=w_scales[:, X, third],
                start=True,
                stop=True,
            )

        def scalar_function(dst, src, lo, hi, func, bias_columns, scale):
            for ut in range(lo // P, hi // P):
                nc.scalar.activation(
                    out=dst[:, ut, :], in_=src[ut], func=func, bias=bias_columns[:, ut : ut + 1], scale=scale
                )

        def by_unit(tile):
            return [tile[:, ut, :] for ut in range(UNIT_TILES)]

        def batch_rows(src, lo, hi, name):
            rows = psum.tile([B, hi - lo], F32, tag="bank", name="%s_%d" % (name, lo))
            for i in range((hi - lo) // P):
                nc.tensor.transpose(rows[:, i * P : (i + 1) * P], src[:, lo // P + i, :], ident_f32[:])
            return rows

        HALVES = ((256, 512), (0, 256))

        x_sb = keep.tile([B, U], BF16)
        h_sb = keep.tile([B, U], BF16)
        bias_rows = keep.tile([P, BIAS_CHUNKS, P], BF16)
        warm_in = keep.tile([P, 1], F32)
        warm_out = keep.tile([P, 1], F32)
        nc.vector.memset(warm_in[:], 0.0)
        nc.scalar.activation(out=warm_out[:], in_=warm_in[:], func=ACT.Tanh)
        nc.vector.memset(bias_rows[:], 0.0)
        load(X, GATE_R)
        nc.sync.dma_start(out=x_sb[:], in_=inputs)
        nc.sync.dma_start(out=h_sb[:], in_=h_tm1)
        nc.sync.dma_start(
            out=bias_rows[0:BIAS_ROWS, :, :].rearrange("r c p -> r (c p)"),
            in_=bias.rearrange("i (r f) -> (i r) f", f=BIAS_CHUNKS * P),
        )
        load(H, GATE_R)
        load(H, GATE_C)
        load(X, GATE_C)
        load(X, GATE_Z)
        load(H, GATE_Z)

        ident_f32 = keep.tile([P, P], F32)
        make_identity(nc, ident_f32[:])
        ident_bf = keep.tile([P, P], BF16)
        make_identity(nc, ident_bf[:])

        x_t = psum.tile([P, 2, B], F32, tag="bank")
        h_t = psum.tile([P, 2, B], F32, tag="bank")
        bias_t = psum.tile([P, BIAS_CHUNKS, P], BF16, tag="bank")
        for words_t, rows in ((x_t, x_sb), (h_t, h_sb)):
            for u in range(2):
                nc.tensor.transpose(words_t[:, u, :], rows[:].bitcast(F32)[:, u : U // 2 : 2], ident_f32[:])
        for c in range(BIAS_CHUNKS):
            nc.tensor.transpose(bias_t[:, c, :], bias_rows[:, c, :], ident_bf[:])

        vector_regroup(X, GATE_R, 0, 256)
        vector_regroup(X, GATE_R, 256, 512)
        for side, words_t in ((X, x_t), (H, h_t)):
            nc.scalar.copy(
                out=act_grouped[:, side, :, :].rearrange("p b t -> p (b t)").bitcast(F32),
                in_=words_t[:].rearrange("p u b -> p b u"),
            )
        bias_cols = keep.tile([P, 2 * 3 * UNIT_TILES], F32)
        nc.scalar.copy(
            out=bias_cols[:].rearrange("p (r c) -> p r c", c=BIAS_CHUNKS),
            in_=bias_t[:, :, 0:BIAS_ROWS].rearrange("p c r -> p r c"),
        )
        quantise(X, GATE_R, 0, 256)
        quantise(X, GATE_R, 256, 512)
        vector_regroup(H, GATE_R, 0, 256)
        scalar_regroup(H, GATE_R, 256, 512)
        nc.vector.quantize_mx(
            out=act_codes[:].rearrange("p s b -> p (s b)").bitcast(FP8X4),
            scales=act_scales[:].rearrange("p s b -> p (s b)"),
            in_=act_grouped[:].rearrange("p s b t -> p (s b t)"),
        )
        gate_shift = keep.tile([P, 2 * UNIT_TILES], F32)
        nc.vector.scalar_tensor_tensor(
            out=gate_shift[:],
            in0=bias_cols[:, 0 : 2 * UNIT_TILES],
            scalar=2.5,
            in1=bias_cols[:, 3 * UNIT_TILES : 5 * UNIT_TILES],
            op0=ALU.add,
            op1=ALU.add,
        )
        rec_cand_bias = keep.tile([P, UNIT_TILES], F32)
        nc.vector.tensor_scalar_mul(
            out=rec_cand_bias[:], in0=bias_cols[:, 5 * UNIT_TILES : 6 * UNIT_TILES], scalar1=0.2
        )
        z_shift = gate_shift[:, 0:UNIT_TILES]
        r_shift = gate_shift[:, UNIT_TILES : 2 * UNIT_TILES]
        cand_bias = bias_cols[:, 2 * UNIT_TILES : 3 * UNIT_TILES]

        acc_r = unit_banks("acc_r")
        gate_pass(acc_r, X, GATE_R, 0, U)
        keep_busy()
        keep_busy()
        vector_regroup(H, GATE_C, 0, 256)
        scalar_regroup(H, GATE_C, 256, 512)
        quantise(H, GATE_R, 0, 512)
        gate_pass(acc_r, H, GATE_R, 0, U)
        keep_busy()

        vector_regroup(X, GATE_C, 0, 320)
        scalar_regroup(X, GATE_C, 320, 512)
        r5 = keep.tile([P, UNIT_TILES, B], F32)
        scalar_function(r5, [acc[:] for acc in acc_r], 0, U, ACT.Relu, r_shift, 1.0)
        quantise(H, GATE_C, 0, 512)
        acc_rec = product(H, GATE_C, "acc_rec")
        keep_busy()

        vector_regroup(X, GATE_Z, 192, 512)
        scalar_regroup(X, GATE_Z, 0, 192)
        rec_fifth = keep.tile([P, UNIT_TILES, B], F32)
        scalar_function(rec_fifth, by_unit(acc_rec), 0, U, ACT.Identity, rec_cand_bias, 0.2)
        quantise(X, GATE_C, 0, 512)
        acc_x = product(X, GATE_C, "acc_x")
        keep_busy()

        quantise(X, GATE_Z, 0, 512)
        acc_z = unit_banks("acc_z")
        for lo, hi in HALVES:
            gate_pass(acc_z, X, GATE_Z, lo, hi)
        keep_busy()
        keep_busy()
        scalar_regroup(H, GATE_Z, 256, 384)
        scalar_regroup(H, GATE_Z, 0, 256)

        gated = keep.tile([P, UNIT_TILES, B], F32)
        pre = keep.tile([P, UNIT_TILES, B], F32)
        for lo, hi in HALVES:
            uts = slice(lo // P, hi // P)
            nc.vector.scalar_tensor_tensor(
                out=gated[:, uts, :], in0=r5[:, uts, :], scalar=5.0, in1=rec_fifth[:, uts, :],
                op0=ALU.min, op1=ALU.mult,
            )
        vector_regroup(H, GATE_Z, 384, 512)
        for lo, hi in HALVES:
            uts = slice(lo // P, hi // P)
            nc.vector.tensor_tensor(
                out=pre[:, uts, :], in0=acc_x[:, uts, :], in1=gated[:, uts, :], op=ALU.add
            )
            quantise(H, GATE_Z, lo, hi)

        hh = keep.tile([P, UNIT_TILES, B], F32)
        z5 = keep.tile([P, UNIT_TILES, B], F32)
        diff = keep.tile([B, U], F32)
        moved = keep.tile([B, U], F32)
        out_sb = keep.tile([B, U], F32)
        hh_rows = []
        for lo, hi in HALVES:
            scalar_function(hh, by_unit(pre), lo, hi, ACT.Tanh, cand_bias, 1.0)
            gate_pass(acc_z, H, GATE_Z, lo, hi)
            hh_rows.append(batch_rows(hh, lo, hi, "hh_rows"))
        z5_rows = []
        for lo, hi in HALVES:
            scalar_function(z5, [acc[:] for acc in acc_z], lo, hi, ACT.Relu, z_shift, 1.0)
            z5_rows.append(batch_rows(z5, lo, hi, "z5_rows"))
        for rows, (lo, hi) in zip(hh_rows, HALVES):
            nc.vector.tensor_tensor(out=diff[:, lo:hi], in0=h_sb[:, lo:hi], in1=rows[:], op=ALU.subtract)
        for rows, (lo, hi) in zip(z5_rows, HALVES):
            nc.vector.scalar_tensor_tensor(
                out=moved[:, lo:hi], in0=rows[:], scalar=5.0, in1=diff[:, lo:hi], op0=ALU.min, op1=ALU.mult
            )
        for rows, (lo, hi) in zip(hh_rows, HALVES):
            nc.vector.scalar_tensor_tensor(
                out=out_sb[:, lo:hi], in0=moved[:, lo:hi], scalar=0.2, in1=rows[:], op0=ALU.mult, op1=ALU.add
            )
            nc.sync.dma_start(out=out[:, lo:hi], in_=out_sb[:, lo:hi])
